import numpy as np
import ml_dtypes


def mxq(x, axis, fmt="e4m3"):
    dtype, down = {"e4m3": (ml_dtypes.float8_e4m3fn, 7), "e5m2": (ml_dtypes.float8_e5m2, 14)}[fmt]
    v = np.moveaxis(np.asarray(x, np.float32).astype(ml_dtypes.bfloat16).astype(np.float64), axis, -1)
    blocks = v.reshape(v.shape[:-1] + (-1, 32))
    amax = np.abs(blocks).max(-1, keepdims=True)
    byte = np.maximum(np.where(amax > 0, np.frexp(amax)[1] - 1 + 127, 0) - down, 1)
    scale = np.exp2(byte - 127.0)
    codes = (blocks / scale).astype(np.float32).astype(dtype).astype(np.float64)
    return np.moveaxis((codes * scale).reshape(v.shape), -1, axis)


WIDE = False


def mx_kscale(k):
    if not WIDE:
        return np.ones(k)
    levels = np.array([10, -10, 5, -5, 0])
    a = np.random.permutation(np.resize(levels, k // 512 * 4)).reshape(k // 512, 4)
    idx = np.arange(k)
    return np.exp2(a[idx // 512, idx % 128 // 32])


BF16 = ml_dtypes.bfloat16


def bf(x):
    return np.asarray(x, np.float32).astype(BF16)


def f64(x):
    return np.asarray(x).astype(np.float64)


E2M1 = np.array([0.0, 0.5, 1.0, 1.5, 2.0, 3.0, 4.0, 6.0, -0.0, -0.5, -1.0, -1.5, -2.0, -3.0, -4.0, -6.0])


def pack_weight(w, fmt):
    k, n = w.shape
    w = f64(bf(w)).reshape(k // 32, 32, n)
    amax = np.abs(w).max(1)
    if fmt == "e4m3":
        byte = np.frexp(amax)[1] - 1 + 127 - 7
    else:
        mant, ex = np.frexp(amax / 6.0)
        byte = np.where(mant > 0.5, ex, ex - 1) + 127
    byte = np.clip(np.where(amax > 0, byte, 1), 1, 254)
    scaled = (w * np.exp2(127.0 - byte)[:, None, :]).reshape(k, n).astype(np.float32)
    by_word = np.ascontiguousarray(scaled.reshape(k // 512, 128, 4, n).transpose(0, 1, 3, 2))
    if fmt == "e4m3":
        words = by_word.astype(ml_dtypes.float8_e4m3fn).view(np.uint8)
    else:
        c = by_word.astype(ml_dtypes.float4_e2m1fn).view(np.uint8) & 0xF
        words = c[..., 0::2] | (c[..., 1::2] << 4)
    return np.ascontiguousarray(words), np.ascontiguousarray(byte.astype(np.uint8).reshape(k // 512, 16, n))


def unpack_weight(words, scales, fmt):
    g, p, n, _ = words.shape
    if fmt == "e4m3":
        vals = np.ascontiguousarray(words).view(ml_dtypes.float8_e4m3fn).astype(np.float64)
    else:
        nib = np.empty((g, p, n, 4), np.uint8)
        nib[..., 0::2] = words & 0xF
        nib[..., 1::2] = words >> 4
        vals = E2M1[nib]
    vals = vals * np.repeat(np.exp2(scales.astype(np.float64) - 127.0), 8, axis=1)[..., None]
    return vals.transpose(0, 1, 3, 2).reshape(g * 512, n)


N, CIN, COUT, V, T, S = 2, 1024, 64, 64, 64, 8
EPS = 1e-5
KG = S * V


def setup_inputs():
    r = np.random.standard_normal
    c = mx_kscale(CIN)
    g = mx_kscale(KG).reshape(S, V)
    ada_A = bf(r((N, CIN, V, V)) * c[None, :, None, None])
    stack = (r((S, COUT, CIN)) / np.sqrt(CIN) / c).swapaxes(1, 2)
    words, scales = pack_weight(stack.reshape(-1, COUT), "e4m3")
    return {"ada_A": ada_A,
            "ada_w_words": words,
            "ada_w_scales": scales,
            "ada_b": bf(r((S, COUT)) * 0.3),
            "PA": bf(r((S, V, V)) * 2.0 / np.sqrt(KG) * g[:, None, :]),
            "feat": bf(r((S, N, COUT, V, T)) / g[:, None, None, :, None]),
            "bn_gamma": bf(1.0 + 0.1 * r(COUT)),
            "bn_beta": bf(0.3 * r(COUT)),
            "bn_mean": bf(0.3 * r(COUT)),
            "bn_var": bf(np.abs(r(COUT)) + 1.0),
            "res": bf(r((N, COUT, V, T)) * 0.9)}


def reference(ada_A, ada_w_words, ada_w_scales, ada_b, PA, feat, bn_gamma, bn_beta, bn_mean, bn_var, res):
    wq = unpack_weight(ada_w_words, ada_w_scales, "e4m3").reshape(S, CIN, COUT).swapaxes(1, 2).reshape(S * COUT, CIN)
    aq = mxq(f64(ada_A).reshape(N, CIN, V * V), 1, "e4m3")
    adaA = (wq @ aq).reshape(N, S, COUT, V, V).transpose(1, 0, 2, 3, 4) + f64(ada_b)[:, None, :, None, None]
    A_full = adaA * f64(PA)[:, None, None, :, :]
    Ag = A_full.transpose(1, 2, 3, 0, 4).reshape(N, COUT, V, KG)
    Fg = f64(feat).transpose(1, 2, 0, 3, 4).reshape(N, COUT, KG, T)
    y = mxq(Ag, 3, "e4m3") @ mxq(Fg, 2, "e4m3")
    scale = f64(bn_gamma) / np.sqrt(f64(bn_var) + EPS)
    z = (y - f64(bn_mean)[:, None, None]) * scale[:, None, None] + f64(bn_beta)[:, None, None]
    return np.maximum(z + f64(res), 0.0)

@@ -1,0 +1,367 @@
+from contextlib import ExitStack
+
+import concourse.masks as masks
+import concourse.mybir as mybir
+
+BF16 = mybir.dt.bfloat16
+F32 = mybir.dt.float32
+I32 = mybir.dt.int32
+U32 = mybir.dt.uint32
+U8 = mybir.dt.uint8
+FP8X4 = mybir.dt.float8_e4m3fn_x4
+ADD = mybir.AluOpType.add
+MULT = mybir.AluOpType.mult
+RELU = mybir.ActivationFunctionType.Relu
+
+P = 128
+PACK = 4
+K_PASS = P * PACK
+SAMPLES, CIN, COUT, JOINTS, FRAMES, SUBSETS = 2, 1024, 64, 64, 64, 8
+EPS = 1e-5
+PASSES = CIN // K_PASS
+Z_TILES = SUBSETS // 2
+HALF = P // 2
+
+CHUNK_V = 16
+CHUNK_COLS = CHUNK_V * JOINTS
+CHUNKS = JOINTS // CHUNK_V
+STEP_V = 8
+STEP_COLS = STEP_V * JOINTS
+STEPS = SAMPLES * JOINTS // STEP_V
+BANK_V = 4
+UNIT_O = 16
+UNITS = COUT // UNIT_O
+BANK_PAIRS = 4
+
+FLOPS = 2 * SUBSETS * COUT * CIN * SAMPLES * JOINTS * JOINTS + 2 * SAMPLES * COUT * JOINTS * SUBSETS * JOINTS * FRAMES
+
+
+def tile_multiscale_gcn_pa_t_e_kernel(
+    tc, ada_A, ada_w_words, ada_w_scales, ada_b, PA, feat, bn_gamma, bn_beta, bn_mean, bn_var, res, out
+):
+    nc = tc.nc
+    with ExitStack() as ctx:
+        ctx.enter_context(tc.manual_schedule())
+        const = ctx.enter_context(tc.tile_pool(name="const", bufs=1))
+        raw_pool = ctx.enter_context(tc.tile_pool(name="raw", bufs=2 * PASSES))
+        grouped_pool = ctx.enter_context(tc.tile_pool(name="grouped", bufs=2))
+        a_pool = ctx.enter_context(tc.tile_pool(name="ada_codes", bufs=3))
+        psum_acc = ctx.enter_context(tc.psum_pool(name="psum_acc", bufs=4))
+        psum_xt = ctx.enter_context(tc.psum_pool(name="psum_xt", bufs=2))
+        psum_y = ctx.enter_context(tc.psum_pool(name="psum_y", bufs=2))
+
+        def load_ada_chunk(chunk):
+            n, vc = divmod(chunk, CHUNKS)
+            tiles = []
+            for h in range(PASSES):
+                raw = raw_pool.tile([P, PACK, CHUNK_COLS], BF16)
+                rows = ada_A[n, h * K_PASS : (h + 1) * K_PASS, vc * CHUNK_V : (vc + 1) * CHUNK_V, :]
+                nc.sync.dma_start(out=raw[:], in_=rows.rearrange("(p j) v w -> p j (v w)", j=PACK))
+                tiles.append(raw)
+            return tiles
+
+        def regroup_ada(step, raws):
+            cols = slice((step % 2) * STEP_COLS, (step % 2 + 1) * STEP_COLS)
+            grouped = grouped_pool.tile([P, PASSES, STEP_COLS, PACK], BF16, align_bytes=64)
+            for h in range(PASSES):
+                nc.scalar.copy(
+                    out=grouped[:, h].rearrange("p (c i) j -> p c j i", i=4),
+                    in_=raws[h][:, :, cols].rearrange("p j (c i) -> p c j i", i=4),
+                )
+            return grouped
+
+        def quantise_ada(grouped):
+            codes = a_pool.tile([P, PASSES, STEP_COLS], U32, align_bytes=64)
+            scales = a_pool.tile([P, PASSES, STEP_COLS], U8, align_bytes=64)
+            nc.vector.quantize_mx(
+                out=codes[:].rearrange("p h c -> p (h c)").bitcast(FP8X4),
+                scales=scales[:].rearrange("p h c -> p (h c)"),
+                in_=grouped[:].rearrange("p h c j -> p (h c j)"),
+            )
+            return codes, scales
+
+        pa_rows = const.tile([P, JOINTS * JOINTS], BF16)
+        pa_all = const.tile([P, Z_TILES, JOINTS * JOINTS], BF16)
+        spread = const.tile([P, Z_TILES, 2, COUT], BF16)
+        ident_bf = const.tile([P, P], BF16)
+        ident_f32 = const.tile([P, P], F32)
+        w_words = const.tile([P, PASSES, Z_TILES, P], U32, align_bytes=64)
+        w_scales = const.tile([P, PASSES, Z_TILES, P], U8, align_bytes=64)
+        bias = const.tile([P, Z_TILES], F32)
+        bn_scale = const.tile([P, COUT // 2], F32)
+        bn_shift = const.tile([P, COUT // 2], F32)
+
+        def spread_pa(step):
+            cols = slice(step * STEP_COLS, (step + 1) * STEP_COLS)
+            for pair in range(Z_TILES // 2):
+                wide = psum_y.tile([P, 2, STEP_COLS], BF16, tag="y")
+                for i in range(2):
+                    nc.tensor.matmul(
+                        out=wide[:, i, :],
+                        lhsT=spread[:, 2 * pair + i].rearrange("p b o -> p (b o)"),
+                        rhs=pa_rows[:, cols],
+                        start=True,
+                        stop=True,
+                    )
+                if pair == 0:
+                    nc.scalar.copy(out=pa_all[:, 0:2, cols], in_=wide[:])
+                else:
+                    nc.vector.tensor_copy(out=pa_all[:, 2:4, cols], in_=wide[:])
+
+        raws = {}
+        with tc.tile_pool(name="setup", bufs=1) as setup:
+            w_in = setup.tile([P, 2 * SUBSETS, COUT], U32)
+            ws_in = setup.tile([P, 2 * SUBSETS, COUT], U8)
+            b_rows = setup.tile([P, P], BF16)
+            bn_in = setup.tile([P, 4, COUT], BF16)
+            rstd = setup.tile([P, COUT], F32)
+            scale_all = setup.tile([P, COUT], F32)
+            shift_all = setup.tile([P, COUT], F32)
+            nc.vector.memset(pa_rows[:].bitcast(I32), 0)
+            nc.vector.memset(ws_in[:].bitcast(I32), 0)
+            nc.vector.memset(b_rows[:], 0.0)
+
+            for i, vec in enumerate((bn_gamma, bn_beta, bn_mean, bn_var)):
+                nc.sync.dma_start(out=bn_in[:, i, :], in_=vec.partition_broadcast(P))
+            raws[0] = load_ada_chunk(0)
+            nc.sync.dma_start(out=pa_rows[0:SUBSETS, :], in_=PA.rearrange("s v w -> s (v w)"))
+            nc.sync.dma_start(
+                out=w_in[:].bitcast(I32), in_=ada_w_words.rearrange("g p n t -> p g (n t)").bitcast(I32)
+            )
+            for quad in range(4):
+                nc.sync.dma_start(
+                    out=ws_in[32 * quad : 32 * quad + 4].bitcast(I32),
+                    in_=ada_w_scales[:, 4 * quad : 4 * quad + 4, :].rearrange("g r n -> r g n").bitcast(I32),
+                )
+            nc.sync.dma_start(
+                out=b_rows[0:Z_TILES, :].rearrange("z (b o) -> z b o", b=2),
+                in_=ada_b.rearrange("(b z) o -> z b o", z=Z_TILES),
+            )
+            raws[1] = load_ada_chunk(1)
+
+            nc.vector.tensor_scalar_add(out=rstd[:], in0=bn_in[:, 3, :], scalar1=EPS)
+            nc.scalar.sqrt(out=rstd[:], in_=rstd[:])
+            nc.vector.reciprocal(out=rstd[:], in_=rstd[:])
+            nc.vector.tensor_mul(out=scale_all[:], in0=bn_in[:, 0, :], in1=rstd[:])
+            nc.vector.tensor_mul(out=shift_all[:], in0=bn_in[:, 2, :], in1=scale_all[:])
+            nc.vector.tensor_sub(out=shift_all[:], in0=bn_in[:, 1, :], in1=shift_all[:])
+            for k in range(2):
+                rows = slice(k * HALF, (k + 1) * HALF)
+                nc.vector.tensor_copy(
+                    out=bn_scale[rows, :], in_=scale_all[rows, :].rearrange("p (q k) -> p q k", k=2)[:, :, k]
+                )
+                nc.vector.tensor_copy(
+                    out=bn_shift[rows, :], in_=shift_all[rows, :].rearrange("p (q k) -> p q k", k=2)[:, :, k]
+                )
+
+            masks.make_identity(nc, ident_bf[:])
+            nc.vector.tensor_copy(out=ident_f32[:], in_=ident_bf[:])
+            nc.vector.tensor_copy(
+                out=spread[:],
+                in_=ident_bf[:, 0:SUBSETS]
+                .rearrange("p (b z) -> p z b", b=2)
+                .unsqueeze(3)
+                .to_broadcast([P, Z_TILES, 2, COUT]),
+            )
+            spread_pa(0)
+
+            for h in range(PASSES):
+                nc.vector.tensor_copy(
+                    out=w_words[:, h].bitcast(I32).rearrange("p z (b c) -> p z b c", b=2),
+                    in_=w_in[:].bitcast(I32).rearrange("p (b z h) c -> p h z b c", b=2, h=PASSES)[:, h],
+                )
+                nc.vector.tensor_copy(
+                    out=w_scales[:, h].bitcast(I32).rearrange("p z (b c) -> p z b c", b=2),
+                    in_=ws_in[:].bitcast(I32).rearrange("p (b z h) c -> p h z b c", b=2, h=PASSES)[:, h],
+                )
+            b_cols = psum_y.tile([P, P], BF16, tag="y")
+            nc.tensor.transpose(out=b_cols[:], in_=b_rows[:], identity=ident_bf[:])
+            nc.vector.tensor_copy(out=bias[:], in_=b_cols[:, 0:Z_TILES])
+
+        f_pool = ctx.enter_context(tc.tile_pool(name="feat_raw", bufs=2))
+        fg_pool = ctx.enter_context(tc.tile_pool(name="feat_grouped", bufs=2))
+        b_pool = ctx.enter_context(tc.tile_pool(name="a_rows", bufs=2))
+        keep = ctx.enter_context(tc.tile_pool(name="keep", bufs=1))
+        tail = ctx.enter_context(tc.tile_pool(name="tail", bufs=4))
+
+        def load_feat_unit(n, unit):
+            f_raw = f_pool.tile([P, UNIT_O, PACK, FRAMES], BF16)
+            for z in range(Z_TILES):
+                for b in range(2):
+                    block = feat[z + Z_TILES * b, n, unit * UNIT_O : (unit + 1) * UNIT_O]
+                    nc.sync.dma_start(
+                        out=f_raw[32 * z : 32 * (z + 1), :, 2 * b : 2 * b + 2, :],
+                        in_=block.rearrange("o (q e) t -> q o e t", e=2),
+                    )
+            return f_raw
+
+        def quantise_feat_half(f_raw, half, codes, scales):
+            some = slice(half * (UNIT_O // 2), (half + 1) * (UNIT_O // 2))
+            f_grouped = fg_pool.tile([P, UNIT_O // 2, FRAMES, PACK], BF16, align_bytes=64)
+            nc.vector.tensor_copy(
+                out=f_grouped[:].rearrange("p o (c i) k -> p o c k i", i=4),
+                in_=f_raw[:, some].rearrange("p o k (c i) -> p o c k i", i=4),
+            )
+            nc.vector.quantize_mx(
+                out=codes[:, some, :].rearrange("p o t -> p (o t)").bitcast(FP8X4),
+                scales=scales[:, some, :].rearrange("p o t -> p (o t)"),
+                in_=f_grouped[:].rearrange("p o t k -> p (o t k)"),
+            )
+
+        def load_residual(n):
+            res_bf = keep.tile([P, COUT // 2, FRAMES], BF16)
+            nc.sync.dma_start(out=res_bf[:], in_=res[n].rearrange("(q k) v t -> (k v) q t", k=2))
+            res_shift = keep.tile([P, COUT // 2, FRAMES], F32)
+            nc.gpsimd.tensor_tensor(
+                out=res_shift[:],
+                in0=res_bf[:],
+                in1=bn_shift[:].unsqueeze(2).to_broadcast([P, COUT // 2, FRAMES]),
+                op=ADD,
+            )
+            return res_shift
+
+        def first_product(step, ada):
+            codes, scales = ada
+            v0 = (step * STEP_V) % JOINTS
+            a_rows = b_pool.tile([P, STEP_V, Z_TILES, JOINTS], BF16)
+            for z in range(Z_TILES):
+                acc = psum_acc.tile([P, STEP_COLS], F32)
+                for h in range(PASSES):
+                    nc.tensor.matmul_mx(
+                        out=acc[:],
+                        lhsT=w_words[:, h, z, :].bitcast(FP8X4),
+                        lhsT_scale=w_scales[:, h, z, :],
+                        rhs=codes[:, h, :].bitcast(FP8X4),
+                        rhs_scale=scales[:, h, :],
+                        start=(h == 0),
+                        stop=(h == PASSES - 1),
+                    )
+                nc.vector.scalar_tensor_tensor(
+                    out=a_rows[:, :, z, :],
+                    in0=acc[:].rearrange("p (v w) -> p v w", w=JOINTS),
+                    scalar=bias[:, z : z + 1],
+                    in1=pa_all[:, z, v0 * JOINTS : (v0 + STEP_V) * JOINTS].rearrange("p (v w) -> p v w", w=JOINTS),
+                    op0=ADD,
+                    op1=MULT,
+                )
+            return a_rows
+
+        def turn(step, a_rows, a_grouped):
+            v0 = (step * STEP_V) % JOINTS
+            words_in = a_rows[:].rearrange("p v z w -> p v (z w)").bitcast(F32)
+            words_out = (
+                a_grouped[:]
+                .rearrange("p o v k -> p (o v k)")
+                .bitcast(F32)
+                .rearrange("p (o v b) -> p o v b", o=COUT, b=2)
+            )
+            for bank in range(STEP_V // BANK_V):
+                turned = psum_xt.tile([P, BANK_V, P], F32)
+                for i in range(BANK_V):
+                    nc.tensor.transpose(
+                        out=turned[:, i, :], in_=words_in[:, bank * BANK_V + i, :], identity=ident_f32[:]
+                    )
+                first = v0 + bank * BANK_V
+                nc.scalar.copy(
+                    out=words_out[:, :, first : first + BANK_V, :],
+                    in_=turned[:].rearrange("p v (b o) -> p o v b", b=2),
+                )
+
+        def quantise_a(a_grouped):
+            units = []
+            for unit in range(UNITS):
+                a_codes = keep.tile([P, UNIT_O * JOINTS], U32, align_bytes=64, tag="a_codes%d" % unit)
+                a_scales = keep.tile([P, UNIT_O * JOINTS], U8, align_bytes=64, tag="a_scales%d" % unit)
+                nc.vector.quantize_mx(
+                    out=a_codes[:].bitcast(FP8X4),
+                    scales=a_scales[:],
+                    in_=a_grouped[:, unit * UNIT_O : (unit + 1) * UNIT_O].rearrange("p o v k -> p (o v k)"),
+                )
+                units.append((a_codes, a_scales))
+            return units
+
+        def second_product(unit, a_unit, f_unit, res_shift):
+            a_codes, a_scales = a_unit
+            f_codes = f_unit[0][:].rearrange("p o t -> p (o t)")
+            f_scales = f_unit[1][:].rearrange("p o t -> p (o t)")
+            sums = []
+            for bank in range(UNIT_O // 2 // BANK_PAIRS):
+                y = psum_y.tile([P, BANK_PAIRS, P], F32, tag="y")
+                for i in range(BANK_PAIRS):
+                    pair = slice((bank * BANK_PAIRS + i) * P, (bank * BANK_PAIRS + i + 1) * P)
+                    nc.tensor.matmul_mx(
+                        out=y[:, i, :],
+                        lhsT=a_codes[:, pair].bitcast(FP8X4),
+                        lhsT_scale=a_scales[:, pair],
+                        rhs=f_codes[:, pair].bitcast(FP8X4),
+                        rhs_scale=f_scales[:, pair],
+                        start=True,
+                        stop=True,
+                    )
+                q0 = unit * (UNIT_O // 2) + bank * BANK_PAIRS
+                z_t = tail.tile([P, BANK_PAIRS, FRAMES], F32)
+                for k in range(2):
+                    rows = slice(k * HALF, (k + 1) * HALF)
+                    nc.vector.tensor_tensor(
+                        out=z_t[rows],
+                        in0=y[rows, :, k * FRAMES : (k + 1) * FRAMES],
+                        in1=bn_scale[rows, q0 : q0 + BANK_PAIRS].unsqueeze(2).to_broadcast([HALF, BANK_PAIRS, FRAMES]),
+                        op=MULT,
+                    )
+                nc.gpsimd.tensor_tensor(out=z_t[:], in0=z_t[:], in1=res_shift[:, q0 : q0 + BANK_PAIRS, :], op=ADD)
+                sums.append((q0, z_t))
+            return sums
+
+        def finish(n, sums):
+            out_n = out[n].rearrange("(q k) v t -> (k v) q t", k=2)
+            for q0, z_t in sums:
+                nc.scalar.activation(out=z_t[:], in_=z_t[:], func=RELU)
+                nc.scalar.dma_start(out=out_n[:, q0 : q0 + BANK_PAIRS, :], in_=z_t[:])
+
+        steps_a_sample = STEPS // SAMPLES
+        grouped = {0: regroup_ada(0, raws[0]), 1: regroup_ada(1, raws[0])}
+        ada = {0: quantise_ada(grouped[0])}
+        f_raws = {0: load_feat_unit(0, 0)}
+        res_shift = load_residual(0)
+        f_units = {}
+        a_rows = {}
+        a_grouped = None
+        a_units = None
+        sums = None
+        for step in range(STEPS + UNITS + 1):
+            if step + 2 < STEPS:
+                grouped[step + 2] = regroup_ada(step + 2, raws[(step + 2) // 2])
+            if sums is not None:
+                finish(sums[0], sums[1])
+                sums = None
+            if step % 2 == 0:
+                chunk = step // 2
+                if chunk + 2 < SAMPLES * CHUNKS:
+                    raws[chunk + 2] = load_ada_chunk(chunk + 2)
+                if chunk + 1 < SAMPLES * UNITS:
+                    f_raws[chunk + 1] = load_feat_unit((chunk + 1) // UNITS, (chunk + 1) % UNITS)
+            if step + 1 < STEPS:
+                ada[step + 1] = quantise_ada(grouped[step + 1])
+            if step < STEPS:
+                a_rows[step] = first_product(step, ada[step])
+            if 1 <= step <= STEPS:
+                if (step - 1) % steps_a_sample == 0:
+                    a_grouped = keep.tile([P, COUT, JOINTS, PACK], BF16, align_bytes=64)
+                turn(step - 1, a_rows[step - 1], a_grouped)
+            if step + 1 < steps_a_sample:
+                spread_pa(step + 1)
+            if step >= steps_a_sample:
+                n, since = divmod(step - steps_a_sample, steps_a_sample)
+                if since == 0:
+                    a_units = quantise_a(a_grouped)
+                if since < UNITS:
+                    sums = (n, second_product(since, a_units[since], f_units[since], res_shift))
+                if since == UNITS and n + 1 < SAMPLES:
+                    res_shift = load_residual(n + 1)
+            if step < STEPS:
+                unit = (step // 2) % UNITS
+                if step % 2 == 0:
+                    f_codes = keep.tile([P, UNIT_O, FRAMES], U32, align_bytes=64, tag="f_codes%d" % unit)
+                    f_scales = keep.tile([P, UNIT_O, FRAMES], U8, align_bytes=64, tag="f_scales%d" % unit)
+                    f_units[unit] = (f_codes, f_scales)
+                quantise_feat_half(f_raws[step // 2], step % 2, f_units[unit][0], f_units[unit][1])

@@ -56,7 +56,7 @@ def tile_multiscale_gcn_pa_t_e_kernel(
             for h in range(PASSES):
                 raw = raw_pool.tile([P, PACK, CHUNK_COLS], BF16)
                 rows = ada_A[n, h * K_PASS : (h + 1) * K_PASS, vc * CHUNK_V : (vc + 1) * CHUNK_V, :]
-                nc.sync.dma_start(out=raw[:], in_=rows.rearrange("(p j) v w -> p j (v w)", j=PACK))
+                nc.scalar.dma_start(out=raw[:], in_=rows.rearrange("(p j) v w -> p j (v w)", j=PACK))
                 tiles.append(raw)
             return tiles
 

@@ -56,15 +56,15 @@ def tile_multiscale_gcn_pa_t_e_kernel(
             for h in range(PASSES):
                 raw = raw_pool.tile([P, PACK, CHUNK_COLS], BF16)
                 rows = ada_A[n, h * K_PASS : (h + 1) * K_PASS, vc * CHUNK_V : (vc + 1) * CHUNK_V, :]
-                nc.scalar.dma_start(out=raw[:], in_=rows.rearrange("(p j) v w -> p j (v w)", j=PACK))
+                nc.sync.dma_start(out=raw[:], in_=rows.rearrange("(p j) v w -> p j (v w)", j=PACK))
                 tiles.append(raw)
             return tiles
 
-        def regroup_ada(step, raws):
+        def regroup_ada(step, raws, copy):
             cols = slice((step % 2) * STEP_COLS, (step % 2 + 1) * STEP_COLS)
             grouped = grouped_pool.tile([P, PASSES, STEP_COLS, PACK], BF16, align_bytes=64)
             for h in range(PASSES):
-                nc.scalar.copy(
+                copy(
                     out=grouped[:, h].rearrange("p (c i) j -> p c j i", i=4),
                     in_=raws[h][:, :, cols].rearrange("p j (c i) -> p c j i", i=4),
                 )
@@ -84,7 +84,7 @@ def tile_multiscale_gcn_pa_t_e_kernel(
         pa_all = const.tile([P, Z_TILES, JOINTS * JOINTS], BF16)
         spread = const.tile([P, Z_TILES, 2, COUT], BF16)
         ident_bf = const.tile([P, P], BF16)
-        ident_f32 = const.tile([P, P], F32)
+        swap_f32 = const.tile([P, P], F32)
         w_words = const.tile([P, PASSES, Z_TILES, P], U32, align_bytes=64)
         w_scales = const.tile([P, PASSES, Z_TILES, P], U8, align_bytes=64)
         bias = const.tile([P, Z_TILES], F32)
@@ -155,7 +155,9 @@ def tile_multiscale_gcn_pa_t_e_kernel(
                 )
 
             masks.make_identity(nc, ident_bf[:])
-            nc.vector.tensor_copy(out=ident_f32[:], in_=ident_bf[:])
+            nc.vector.tensor_copy(
+                out=swap_f32[:].rearrange("p (o b) -> p o b", b=2), in_=ident_bf[:].rearrange("p (b o) -> p o b", b=2)
+            )
             nc.vector.tensor_copy(
                 out=spread[:],
                 in_=ident_bf[:, 0:SUBSETS]
@@ -164,6 +166,12 @@ def tile_multiscale_gcn_pa_t_e_kernel(
                 .to_broadcast([P, Z_TILES, 2, COUT]),
             )
             spread_pa(0)
+
+            grouped = {
+                0: regroup_ada(0, raws[0], nc.vector.tensor_copy),
+                1: regroup_ada(1, raws[0], nc.vector.tensor_copy),
+            }
+            ada = {0: quantise_ada(grouped[0])}
 
             for h in range(PASSES):
                 nc.vector.tensor_copy(
@@ -179,7 +187,7 @@ def tile_multiscale_gcn_pa_t_e_kernel(
             nc.vector.tensor_copy(out=bias[:], in_=b_cols[:, 0:Z_TILES])
 
         f_pool = ctx.enter_context(tc.tile_pool(name="feat_raw", bufs=2))
-        fg_pool = ctx.enter_context(tc.tile_pool(name="feat_grouped", bufs=2))
+        fg_pool = ctx.enter_context(tc.tile_pool(name="feat_grouped", bufs=1))
         b_pool = ctx.enter_context(tc.tile_pool(name="a_rows", bufs=2))
         keep = ctx.enter_context(tc.tile_pool(name="keep", bufs=1))
         tail = ctx.enter_context(tc.tile_pool(name="tail", bufs=4))
@@ -195,30 +203,31 @@ def tile_multiscale_gcn_pa_t_e_kernel(
                     )
             return f_raw
 
-        def quantise_feat_half(f_raw, half, codes, scales):
+        def regroup_feat(f_raw, half):
             some = slice(half * (UNIT_O // 2), (half + 1) * (UNIT_O // 2))
             f_grouped = fg_pool.tile([P, UNIT_O // 2, FRAMES, PACK], BF16, align_bytes=64)
-            nc.vector.tensor_copy(
-                out=f_grouped[:].rearrange("p o (c i) k -> p o c k i", i=4),
-                in_=f_raw[:, some].rearrange("p o k (c i) -> p o c k i", i=4),
+            nc.gpsimd.tensor_scalar(
+                out=f_grouped[:],
+                in0=f_raw[:, some].rearrange("p o k t -> p o t k"),
+                scalar1=1.0,
+                scalar2=0.0,
+                op0=MULT,
+                op1=ADD,
             )
+            return f_grouped
+
+        def quantise_feat(f_grouped, half, f_unit):
+            some = slice(half * (UNIT_O // 2), (half + 1) * (UNIT_O // 2))
             nc.vector.quantize_mx(
-                out=codes[:, some, :].rearrange("p o t -> p (o t)").bitcast(FP8X4),
-                scales=scales[:, some, :].rearrange("p o t -> p (o t)"),
+                out=f_unit[0][:, some, :].rearrange("p o t -> p (o t)").bitcast(FP8X4),
+                scales=f_unit[1][:, some, :].rearrange("p o t -> p (o t)"),
                 in_=f_grouped[:].rearrange("p o t k -> p (o t k)"),
             )
 
         def load_residual(n):
             res_bf = keep.tile([P, COUT // 2, FRAMES], BF16)
             nc.sync.dma_start(out=res_bf[:], in_=res[n].rearrange("(q k) v t -> (k v) q t", k=2))
-            res_shift = keep.tile([P, COUT // 2, FRAMES], F32)
-            nc.gpsimd.tensor_tensor(
-                out=res_shift[:],
-                in0=res_bf[:],
-                in1=bn_shift[:].unsqueeze(2).to_broadcast([P, COUT // 2, FRAMES]),
-                op=ADD,
-            )
-            return res_shift
+            return res_bf
 
         def first_product(step, ada):
             codes, scales = ada
@@ -259,12 +268,12 @@ def tile_multiscale_gcn_pa_t_e_kernel(
                 turned = psum_xt.tile([P, BANK_V, P], F32)
                 for i in range(BANK_V):
                     nc.tensor.transpose(
-                        out=turned[:, i, :], in_=words_in[:, bank * BANK_V + i, :], identity=ident_f32[:]
+                        out=turned[:, i, :], in_=words_in[:, bank * BANK_V + i, :], identity=swap_f32[:]
                     )
                 first = v0 + bank * BANK_V
                 nc.scalar.copy(
                     out=words_out[:, :, first : first + BANK_V, :],
-                    in_=turned[:].rearrange("p v (b o) -> p o v b", b=2),
+                    in_=turned[:].rearrange("p v (o b) -> p o v b", b=2),
                 )
 
         def quantise_a(a_grouped):
@@ -280,7 +289,7 @@ def tile_multiscale_gcn_pa_t_e_kernel(
                 units.append((a_codes, a_scales))
             return units
 
-        def second_product(unit, a_unit, f_unit, res_shift):
+        def second_product(unit, a_unit, f_unit, res_bf):
             a_codes, a_scales = a_unit
             f_codes = f_unit[0][:].rearrange("p o t -> p (o t)")
             f_scales = f_unit[1][:].rearrange("p o t -> p (o t)")
@@ -308,29 +317,31 @@ def tile_multiscale_gcn_pa_t_e_kernel(
                         in1=bn_scale[rows, q0 : q0 + BANK_PAIRS].unsqueeze(2).to_broadcast([HALF, BANK_PAIRS, FRAMES]),
                         op=MULT,
                     )
-                nc.gpsimd.tensor_tensor(out=z_t[:], in0=z_t[:], in1=res_shift[:, q0 : q0 + BANK_PAIRS, :], op=ADD)
+                nc.gpsimd.tensor_tensor(out=z_t[:], in0=z_t[:], in1=res_bf[:, q0 : q0 + BANK_PAIRS, :], op=ADD)
                 sums.append((q0, z_t))
             return sums
 
         def finish(n, sums):
             out_n = out[n].rearrange("(q k) v t -> (k v) q t", k=2)
             for q0, z_t in sums:
-                nc.scalar.activation(out=z_t[:], in_=z_t[:], func=RELU)
+                for i in range(BANK_PAIRS):
+                    nc.scalar.activation(
+                        out=z_t[:, i, :], in_=z_t[:, i, :], func=RELU, bias=bn_shift[:, q0 + i : q0 + i + 1]
+                    )
                 nc.scalar.dma_start(out=out_n[:, q0 : q0 + BANK_PAIRS, :], in_=z_t[:])
 
         steps_a_sample = STEPS // SAMPLES
-        grouped = {0: regroup_ada(0, raws[0]), 1: regroup_ada(1, raws[0])}
-        ada = {0: quantise_ada(grouped[0])}
         f_raws = {0: load_feat_unit(0, 0)}
-        res_shift = load_residual(0)
         f_units = {}
+        f_grouped = None
         a_rows = {}
         a_grouped = None
         a_units = None
+        res_bf = None
         sums = None
         for step in range(STEPS + UNITS + 1):
             if step + 2 < STEPS:
-                grouped[step + 2] = regroup_ada(step + 2, raws[(step + 2) // 2])
+                grouped[step + 2] = regroup_ada(step + 2, raws[(step + 2) // 2], nc.scalar.copy)
             if sums is not None:
                 finish(sums[0], sums[1])
                 sums = None
@@ -342,7 +353,15 @@ def tile_multiscale_gcn_pa_t_e_kernel(
                     f_raws[chunk + 1] = load_feat_unit((chunk + 1) // UNITS, (chunk + 1) % UNITS)
             if step + 1 < STEPS:
                 ada[step + 1] = quantise_ada(grouped[step + 1])
+            if 1 <= step <= STEPS:
+                unit = ((step - 1) // 2) % UNITS
+                if (step - 1) % 2 == 0:
+                    f_codes = keep.tile([P, UNIT_O, FRAMES], U32, align_bytes=64, tag="f_codes%d" % unit)
+                    f_scales = keep.tile([P, UNIT_O, FRAMES], U8, align_bytes=64, tag="f_scales%d" % unit)
+                    f_units[unit] = (f_codes, f_scales)
+                quantise_feat(f_grouped, (step - 1) % 2, f_units[unit])
             if step < STEPS:
+                f_grouped = regroup_feat(f_raws[step // 2], step % 2)
                 a_rows[step] = first_product(step, ada[step])
             if 1 <= step <= STEPS:
                 if (step - 1) % steps_a_sample == 0:
@@ -350,18 +369,11 @@ def tile_multiscale_gcn_pa_t_e_kernel(
                 turn(step - 1, a_rows[step - 1], a_grouped)
             if step + 1 < steps_a_sample:
                 spread_pa(step + 1)
+            if step < STEPS and step % steps_a_sample == UNITS:
+                res_bf = load_residual(step // steps_a_sample)
             if step >= steps_a_sample:
                 n, since = divmod(step - steps_a_sample, steps_a_sample)
                 if since == 0:
                     a_units = quantise_a(a_grouped)
                 if since < UNITS:
-                    sums = (n, second_product(since, a_units[since], f_units[since], res_shift))
-                if since == UNITS and n + 1 < SAMPLES:
-                    res_shift = load_residual(n + 1)
-            if step < STEPS:
-                unit = (step // 2) % UNITS
-                if step % 2 == 0:
-                    f_codes = keep.tile([P, UNIT_O, FRAMES], U32, align_bytes=64, tag="f_codes%d" % unit)
-                    f_scales = keep.tile([P, UNIT_O, FRAMES], U8, align_bytes=64, tag="f_scales%d" % unit)
-                    f_units[unit] = (f_codes, f_scales)
-                quantise_feat_half(f_raws[step // 2], step % 2, f_units[unit][0], f_units[unit][1])
+                    sums = (n, second_product(since, a_units[since], f_units[since], res_bf))

from contextlib import ExitStack

import concourse.masks as masks
import concourse.mybir as mybir

BF16 = mybir.dt.bfloat16
F32 = mybir.dt.float32
I32 = mybir.dt.int32
U32 = mybir.dt.uint32
U8 = mybir.dt.uint8
FP8X4 = mybir.dt.float8_e4m3fn_x4
ADD = mybir.AluOpType.add
MULT = mybir.AluOpType.mult
RELU = mybir.ActivationFunctionType.Relu

P = 128
PACK = 4
K_PASS = P * PACK
SAMPLES, CIN, COUT, JOINTS, FRAMES, SUBSETS = 2, 1024, 64, 64, 64, 8
EPS = 1e-5
PASSES = CIN // K_PASS
Z_TILES = SUBSETS // 2
HALF = P // 2

CHUNK_V = 16
CHUNK_COLS = CHUNK_V * JOINTS
CHUNKS = JOINTS // CHUNK_V
STEP_V = 8
STEP_COLS = STEP_V * JOINTS
STEPS = SAMPLES * JOINTS // STEP_V
BANK_V = 4
UNIT_O = 16
UNITS = COUT // UNIT_O
BANK_PAIRS = 4

FLOPS = 2 * SUBSETS * COUT * CIN * SAMPLES * JOINTS * JOINTS + 2 * SAMPLES * COUT * JOINTS * SUBSETS * JOINTS * FRAMES


def tile_multiscale_gcn_pa_t_e_kernel(
    tc, ada_A, ada_w_words, ada_w_scales, ada_b, PA, feat, bn_gamma, bn_beta, bn_mean, bn_var, res, out
):
    nc = tc.nc
    with ExitStack() as ctx:
        ctx.enter_context(tc.manual_schedule())
        const = ctx.enter_context(tc.tile_pool(name="const", bufs=1))
        raw_pool = ctx.enter_context(tc.tile_pool(name="raw", bufs=2 * PASSES))
        grouped_pool = ctx.enter_context(tc.tile_pool(name="grouped", bufs=2))
        a_pool = ctx.enter_context(tc.tile_pool(name="ada_codes", bufs=3))
        psum_acc = ctx.enter_context(tc.psum_pool(name="psum_acc", bufs=4))
        psum_xt = ctx.enter_context(tc.psum_pool(name="psum_xt", bufs=2))
        psum_y = ctx.enter_context(tc.psum_pool(name="psum_y", bufs=2))

        def load_ada_chunk(chunk):
            n, vc = divmod(chunk, CHUNKS)
            tiles = []
            for h in range(PASSES):
                raw = raw_pool.tile([P, PACK, CHUNK_COLS], BF16)
                rows = ada_A[n, h * K_PASS : (h + 1) * K_PASS, vc * CHUNK_V : (vc + 1) * CHUNK_V, :]
                nc.sync.dma_start(out=raw[:], in_=rows.rearrange("(p j) v w -> p j (v w)", j=PACK))
                tiles.append(raw)
            return tiles

        def regroup_ada(step, raws, copy):
            cols = slice((step % 2) * STEP_COLS, (step % 2 + 1) * STEP_COLS)
            grouped = grouped_pool.tile([P, PASSES, STEP_COLS, PACK], BF16, align_bytes=64)
            for h in range(PASSES):
                copy(
                    out=grouped[:, h].rearrange("p (c i) j -> p c j i", i=4),
                    in_=raws[h][:, :, cols].rearrange("p j (c i) -> p c j i", i=4),
                )
            return grouped

        def quantise_ada(grouped):
            codes = a_pool.tile([P, PASSES, STEP_COLS], U32, align_bytes=64)
            scales = a_pool.tile([P, PASSES, STEP_COLS], U8, align_bytes=64)
            nc.vector.quantize_mx(
                out=codes[:].rearrange("p h c -> p (h c)").bitcast(FP8X4),
                scales=scales[:].rearrange("p h c -> p (h c)"),
                in_=grouped[:].rearrange("p h c j -> p (h c j)"),
            )
            return codes, scales

        pa_rows = const.tile([P, JOINTS * JOINTS], BF16)
        pa_all = const.tile([P, Z_TILES, JOINTS * JOINTS], BF16)
        spread = const.tile([P, Z_TILES, 2, COUT], BF16)
        ident_bf = const.tile([P, P], BF16)
        swap_f32 = const.tile([P, P], F32)
        w_words = const.tile([P, PASSES, Z_TILES, P], U32, align_bytes=64)
        w_scales = const.tile([P, PASSES, Z_TILES, P], U8, align_bytes=64)
        bias = const.tile([P, Z_TILES], F32)
        bn_scale = const.tile([P, COUT // 2], F32)
        bn_shift = const.tile([P, COUT // 2], F32)

        def spread_pa(step):
            cols = slice(step * STEP_COLS, (step + 1) * STEP_COLS)
            for pair in range(Z_TILES // 2):
                wide = psum_y.tile([P, 2, STEP_COLS], BF16, tag="y")
                for i in range(2):
                    nc.tensor.matmul(
                        out=wide[:, i, :],
                        lhsT=spread[:, 2 * pair + i].rearrange("p b o -> p (b o)"),
                        rhs=pa_rows[:, cols],
                        start=True,
                        stop=True,
                    )
                if pair == 0:
                    nc.scalar.copy(out=pa_all[:, 0:2, cols], in_=wide[:])
                else:
                    nc.vector.tensor_copy(out=pa_all[:, 2:4, cols], in_=wide[:])

        raws = {}
        with tc.tile_pool(name="setup", bufs=1) as setup:
            w_in = setup.tile([P, 2 * SUBSETS, COUT], U32)
            ws_in = setup.tile([P, 2 * SUBSETS, COUT], U8)
            b_rows = setup.tile([P, P], BF16)
            bn_in = setup.tile([P, 4, COUT], BF16)
            rstd = setup.tile([P, COUT], F32)
            scale_all = setup.tile([P, COUT], F32)
            shift_all = setup.tile([P, COUT], F32)
            nc.vector.memset(pa_rows[:].bitcast(I32), 0)
            nc.vector.memset(ws_in[:].bitcast(I32), 0)
            nc.vector.memset(b_rows[:], 0.0)

            for i, vec in enumerate((bn_gamma, bn_beta, bn_mean, bn_var)):
                nc.sync.dma_start(out=bn_in[:, i, :], in_=vec.partition_broadcast(P))
            raws[0] = load_ada_chunk(0)
            nc.sync.dma_start(out=pa_rows[0:SUBSETS, :], in_=PA.rearrange("s v w -> s (v w)"))
            nc.sync.dma_start(
                out=w_in[:].bitcast(I32), in_=ada_w_words.rearrange("g p n t -> p g (n t)").bitcast(I32)
            )
            for quad in range(4):
                nc.sync.dma_start(
                    out=ws_in[32 * quad : 32 * quad + 4].bitcast(I32),
                    in_=ada_w_scales[:, 4 * quad : 4 * quad + 4, :].rearrange("g r n -> r g n").bitcast(I32),
                )
            nc.sync.dma_start(
                out=b_rows[0:Z_TILES, :].rearrange("z (b o) -> z b o", b=2),
                in_=ada_b.rearrange("(b z) o -> z b o", z=Z_TILES),
            )
            raws[1] = load_ada_chunk(1)

            nc.vector.tensor_scalar_add(out=rstd[:], in0=bn_in[:, 3, :], scalar1=EPS)
            nc.scalar.sqrt(out=rstd[:], in_=rstd[:])
            nc.vector.reciprocal(out=rstd[:], in_=rstd[:])
            nc.vector.tensor_mul(out=scale_all[:], in0=bn_in[:, 0, :], in1=rstd[:])
            nc.vector.tensor_mul(out=shift_all[:], in0=bn_in[:, 2, :], in1=scale_all[:])
            nc.vector.tensor_sub(out=shift_all[:], in0=bn_in[:, 1, :], in1=shift_all[:])
            for k in range(2):
                rows = slice(k * HALF, (k + 1) * HALF)
                nc.vector.tensor_copy(
                    out=bn_scale[rows, :], in_=scale_all[rows, :].rearrange("p (q k) -> p q k", k=2)[:, :, k]
                )
                nc.vector.tensor_copy(
                    out=bn_shift[rows, :], in_=shift_all[rows, :].rearrange("p (q k) -> p q k", k=2)[:, :, k]
                )

            masks.make_identity(nc, ident_bf[:])
            nc.vector.tensor_copy(
                out=swap_f32[:].rearrange("p (o b) -> p o b", b=2), in_=ident_bf[:].rearrange("p (b o) -> p o b", b=2)
            )
            nc.vector.tensor_copy(
                out=spread[:],
                in_=ident_bf[:, 0:SUBSETS]
                .rearrange("p (b z) -> p z b", b=2)
                .unsqueeze(3)
                .to_broadcast([P, Z_TILES, 2, COUT]),
            )
            spread_pa(0)

            grouped = {
                0: regroup_ada(0, raws[0], nc.vector.tensor_copy),
                1: regroup_ada(1, raws[0], nc.vector.tensor_copy),
            }
            ada = {0: quantise_ada(grouped[0])}

            for h in range(PASSES):
                nc.vector.tensor_copy(
                    out=w_words[:, h].bitcast(I32).rearrange("p z (b c) -> p z b c", b=2),
                    in_=w_in[:].bitcast(I32).rearrange("p (b z h) c -> p h z b c", b=2, h=PASSES)[:, h],
                )
                nc.vector.tensor_copy(
                    out=w_scales[:, h].bitcast(I32).rearrange("p z (b c) -> p z b c", b=2),
                    in_=ws_in[:].bitcast(I32).rearrange("p (b z h) c -> p h z b c", b=2, h=PASSES)[:, h],
                )
            b_cols = psum_y.tile([P, P], BF16, tag="y")
            nc.tensor.transpose(out=b_cols[:], in_=b_rows[:], identity=ident_bf[:])
            nc.vector.tensor_copy(out=bias[:], in_=b_cols[:, 0:Z_TILES])

        f_pool = ctx.enter_context(tc.tile_pool(name="feat_raw", bufs=2))
        fg_pool = ctx.enter_context(tc.tile_pool(name="feat_grouped", bufs=1))
        b_pool = ctx.enter_context(tc.tile_pool(name="a_rows", bufs=2))
        keep = ctx.enter_context(tc.tile_pool(name="keep", bufs=1))
        tail = ctx.enter_context(tc.tile_pool(name="tail", bufs=4))

        def load_feat_unit(n, unit):
            f_raw = f_pool.tile([P, UNIT_O, PACK, FRAMES], BF16)
            for z in range(Z_TILES):
                for b in range(2):
                    block = feat[z + Z_TILES * b, n, unit * UNIT_O : (unit + 1) * UNIT_O]
                    nc.sync.dma_start(
                        out=f_raw[32 * z : 32 * (z + 1), :, 2 * b : 2 * b + 2, :],
                        in_=block.rearrange("o (q e) t -> q o e t", e=2),
                    )
            return f_raw

        def regroup_feat(f_raw, half):
            some = slice(half * (UNIT_O // 2), (half + 1) * (UNIT_O // 2))
            f_grouped = fg_pool.tile([P, UNIT_O // 2, FRAMES, PACK], BF16, align_bytes=64)
            nc.gpsimd.tensor_scalar(
                out=f_grouped[:],
                in0=f_raw[:, some].rearrange("p o k t -> p o t k"),
                scalar1=1.0,
                scalar2=0.0,
                op0=MULT,
                op1=ADD,
            )
            return f_grouped

        def quantise_feat(f_grouped, half, f_unit):
            some = slice(half * (UNIT_O // 2), (half + 1) * (UNIT_O // 2))
            nc.vector.quantize_mx(
                out=f_unit[0][:, some, :].rearrange("p o t -> p (o t)").bitcast(FP8X4),
                scales=f_unit[1][:, some, :].rearrange("p o t -> p (o t)"),
                in_=f_grouped[:].rearrange("p o t k -> p (o t k)"),
            )

        def load_residual(n):
            res_bf = keep.tile([P, COUT // 2, FRAMES], BF16)
            nc.sync.dma_start(out=res_bf[:], in_=res[n].rearrange("(q k) v t -> (k v) q t", k=2))
            return res_bf

        def first_product(step, ada):
            codes, scales = ada
            v0 = (step * STEP_V) % JOINTS
            a_rows = b_pool.tile([P, STEP_V, Z_TILES, JOINTS], BF16)
            for z in range(Z_TILES):
                acc = psum_acc.tile([P, STEP_COLS], F32)
                for h in range(PASSES):
                    nc.tensor.matmul_mx(
                        out=acc[:],
                        lhsT=w_words[:, h, z, :].bitcast(FP8X4),
                        lhsT_scale=w_scales[:, h, z, :],
                        rhs=codes[:, h, :].bitcast(FP8X4),
                        rhs_scale=scales[:, h, :],
                        start=(h == 0),
                        stop=(h == PASSES - 1),
                    )
                nc.vector.scalar_tensor_tensor(
                    out=a_rows[:, :, z, :],
                    in0=acc[:].rearrange("p (v w) -> p v w", w=JOINTS),
                    scalar=bias[:, z : z + 1],
                    in1=pa_all[:, z, v0 * JOINTS : (v0 + STEP_V) * JOINTS].rearrange("p (v w) -> p v w", w=JOINTS),
                    op0=ADD,
                    op1=MULT,
                )
            return a_rows

        def turn(step, a_rows, a_grouped):
            v0 = (step * STEP_V) % JOINTS
            words_in = a_rows[:].rearrange("p v z w -> p v (z w)").bitcast(F32)
            words_out = (
                a_grouped[:]
                .rearrange("p o v k -> p (o v k)")
                .bitcast(F32)
                .rearrange("p (o v b) -> p o v b", o=COUT, b=2)
            )
            for bank in range(STEP_V // BANK_V):
                turned = psum_xt.tile([P, BANK_V, P], F32)
                for i in range(BANK_V):
                    nc.tensor.transpose(
                        out=turned[:, i, :], in_=words_in[:, bank * BANK_V + i, :], identity=swap_f32[:]
                    )
                first = v0 + bank * BANK_V
                nc.scalar.copy(
                    out=words_out[:, :, first : first + BANK_V, :],
                    in_=turned[:].rearrange("p v (o b) -> p o v b", b=2),
                )

        def quantise_a(a_grouped):
            units = []
            for unit in range(UNITS):
                a_codes = keep.tile([P, UNIT_O * JOINTS], U32, align_bytes=64, tag="a_codes%d" % unit)
                a_scales = keep.tile([P, UNIT_O * JOINTS], U8, align_bytes=64, tag="a_scales%d" % unit)
                nc.vector.quantize_mx(
                    out=a_codes[:].bitcast(FP8X4),
                    scales=a_scales[:],
                    in_=a_grouped[:, unit * UNIT_O : (unit + 1) * UNIT_O].rearrange("p o v k -> p (o v k)"),
                )
                units.append((a_codes, a_scales))
            return units

        def second_product(unit, a_unit, f_unit, res_bf):
            a_codes, a_scales = a_unit
            f_codes = f_unit[0][:].rearrange("p o t -> p (o t)")
            f_scales = f_unit[1][:].rearrange("p o t -> p (o t)")
            sums = []
            for bank in range(UNIT_O // 2 // BANK_PAIRS):
                y = psum_y.tile([P, BANK_PAIRS, P], F32, tag="y")
                for i in range(BANK_PAIRS):
                    pair = slice((bank * BANK_PAIRS + i) * P, (bank * BANK_PAIRS + i + 1) * P)
                    nc.tensor.matmul_mx(
                        out=y[:, i, :],
                        lhsT=a_codes[:, pair].bitcast(FP8X4),
                        lhsT_scale=a_scales[:, pair],
                        rhs=f_codes[:, pair].bitcast(FP8X4),
                        rhs_scale=f_scales[:, pair],
                        start=True,
                        stop=True,
                    )
                q0 = unit * (UNIT_O // 2) + bank * BANK_PAIRS
                z_t = tail.tile([P, BANK_PAIRS, FRAMES], F32)
                for k in range(2):
                    rows = slice(k * HALF, (k + 1) * HALF)
                    nc.vector.tensor_tensor(
                        out=z_t[rows],
                        in0=y[rows, :, k * FRAMES : (k + 1) * FRAMES],
                        in1=bn_scale[rows, q0 : q0 + BANK_PAIRS].unsqueeze(2).to_broadcast([HALF, BANK_PAIRS, FRAMES]),
                        op=MULT,
                    )
                nc.gpsimd.tensor_tensor(out=z_t[:], in0=z_t[:], in1=res_bf[:, q0 : q0 + BANK_PAIRS, :], op=ADD)
                sums.append((q0, z_t))
            return sums

        def finish(n, sums):
            out_n = out[n].rearrange("(q k) v t -> (k v) q t", k=2)
            for q0, z_t in sums:
                for i in range(BANK_PAIRS):
                    nc.scalar.activation(
                        out=z_t[:, i, :], in_=z_t[:, i, :], func=RELU, bias=bn_shift[:, q0 + i : q0 + i + 1]
                    )
                nc.scalar.dma_start(out=out_n[:, q0 : q0 + BANK_PAIRS, :], in_=z_t[:])

        steps_a_sample = STEPS // SAMPLES
        f_raws = {0: load_feat_unit(0, 0)}
        f_units = {}
        f_grouped = None
        a_rows = {}
        a_grouped = None
        a_units = None
        res_bf = None
        sums = None
        for step in range(STEPS + UNITS + 1):
            if step + 2 < STEPS:
                grouped[step + 2] = regroup_ada(step + 2, raws[(step + 2) // 2], nc.scalar.copy)
            if sums is not None:
                finish(sums[0], sums[1])
                sums = None
            if step % 2 == 0:
                chunk = step // 2
                if chunk + 2 < SAMPLES * CHUNKS:
                    raws[chunk + 2] = load_ada_chunk(chunk + 2)
                if chunk + 1 < SAMPLES * UNITS:
                    f_raws[chunk + 1] = load_feat_unit((chunk + 1) // UNITS, (chunk + 1) % UNITS)
            if step + 1 < STEPS:
                ada[step + 1] = quantise_ada(grouped[step + 1])
            if 1 <= step <= STEPS:
                unit = ((step - 1) // 2) % UNITS
                if (step - 1) % 2 == 0:
                    f_codes = keep.tile([P, UNIT_O, FRAMES], U32, align_bytes=64, tag="f_codes%d" % unit)
                    f_scales = keep.tile([P, UNIT_O, FRAMES], U8, align_bytes=64, tag="f_scales%d" % unit)
                    f_units[unit] = (f_codes, f_scales)
                quantise_feat(f_grouped, (step - 1) % 2, f_units[unit])
            if step < STEPS:
                f_grouped = regroup_feat(f_raws[step // 2], step % 2)
                a_rows[step] = first_product(step, ada[step])
            if 1 <= step <= STEPS:
                if (step - 1) % steps_a_sample == 0:
                    a_grouped = keep.tile([P, COUT, JOINTS, PACK], BF16, align_bytes=64)
                turn(step - 1, a_rows[step - 1], a_grouped)
            if step + 1 < steps_a_sample:
                spread_pa(step + 1)
            if step < STEPS and step % steps_a_sample == UNITS:
                res_bf = load_residual(step // steps_a_sample)
            if step >= steps_a_sample:
                n, since = divmod(step - steps_a_sample, steps_a_sample)
                if since == 0:
                    a_units = quantise_a(a_grouped)
                if since < UNITS:
                    sums = (n, second_product(since, a_units[since], f_units[since], res_bf))
